import numpy as np
import ml_dtypes


def mxq(x, axis, fmt="e4m3"):
    dtype, down = {"e4m3": (ml_dtypes.float8_e4m3fn, 7), "e5m2": (ml_dtypes.float8_e5m2, 14)}[fmt]
    v = np.moveaxis(np.asarray(x, np.float32).astype(ml_dtypes.bfloat16).astype(np.float64), axis, -1)
    blocks = v.reshape(v.shape[:-1] + (-1, 32))
    amax = np.abs(blocks).max(-1, keepdims=True)
    byte = np.maximum(np.where(amax > 0, np.frexp(amax)[1] - 1 + 127, 0) - down, 1)
    scale = np.exp2(byte - 127.0)
    codes = (blocks / scale).astype(np.float32).astype(dtype).astype(np.float64)
    return np.moveaxis((codes * scale).reshape(v.shape), -1, axis)


WIDE = False


def mx_kscale(k):
    if not WIDE:
        return np.ones(k)
    levels = np.array([30, -30])
    if k % 512:
        return np.exp2(np.random.permutation(np.resize(levels, k // 32))).repeat(32)
    a = np.empty((k // 512, 16))
    for p in range(k // 512):
        a[p, :8] = np.random.permutation(np.resize(levels, 8))
        for g in range(8):
            far = levels[np.abs(levels - a[p, g]) >= 10]
            a[p, g + 8] = far[np.random.randint(len(far))]
    return np.exp2(a.ravel()).repeat(32)


BF16 = ml_dtypes.bfloat16


def bf(x):
    return np.asarray(x, np.float32).astype(BF16)


def f64(x):
    return np.asarray(x).astype(np.float64)


E2M1 = np.array([0.0, 0.5, 1.0, 1.5, 2.0, 3.0, 4.0, 6.0, -0.0, -0.5, -1.0, -1.5, -2.0, -3.0, -4.0, -6.0])


def pack_weight(w, fmt):
    k, n = w.shape
    w = f64(bf(w)).reshape(k // 32, 32, n)
    amax = np.abs(w).max(1)
    if fmt == "e4m3":
        byte = np.frexp(amax)[1] - 1 + 127 - 7
    else:
        mant, ex = np.frexp(amax / 6.0)
        byte = np.where(mant > 0.5, ex, ex - 1) + 127
    byte = np.clip(np.where(amax > 0, byte, 1), 1, 254)
    scaled = (w * np.exp2(127.0 - byte)[:, None, :]).reshape(k, n).astype(np.float32)
    by_word = np.ascontiguousarray(scaled.reshape(k // 512, 128, 4, n).transpose(0, 1, 3, 2))
    if fmt == "e4m3":
        words = by_word.astype(ml_dtypes.float8_e4m3fn).view(np.uint8)
    else:
        c = by_word.astype(ml_dtypes.float4_e2m1fn).view(np.uint8) & 0xF
        words = c[..., 0::2] | (c[..., 1::2] << 4)
    return np.ascontiguousarray(words), np.ascontiguousarray(byte.astype(np.uint8).reshape(k // 512, 16, n))


def unpack_weight(words, scales, fmt):
    g, p, n, _ = words.shape
    if fmt == "e4m3":
        vals = np.ascontiguousarray(words).view(ml_dtypes.float8_e4m3fn).astype(np.float64)
    else:
        nib = np.empty((g, p, n, 4), np.uint8)
        nib[..., 0::2] = words & 0xF
        nib[..., 1::2] = words >> 4
        vals = E2M1[nib]
    vals = vals * np.repeat(np.exp2(scales.astype(np.float64) - 127.0), 8, axis=1)[..., None]
    return vals.transpose(0, 1, 3, 2).reshape(g * 512, n)

def pack4(w):
    words, scales = pack_weight(w, "e2m1")
    return words.reshape(words.shape[0], 128, -1), scales


def unpack4(words, scales):
    return unpack_weight(words.reshape(words.shape[0], 128, -1, 2), scales, "e2m1")


B, CIN, P, COUT, W, H, HEADS = 2, 1024, 512, 2048, 16, 32, 4
N = W * H
EPS = 1e-5


def bn(y, g, b, m, v):
    return (y - f64(m)[None, :, None]) * (f64(g) / np.sqrt(f64(v) + EPS))[None, :, None] + f64(b)[None, :, None]


def setup_inputs():
    s, t = mx_kscale(P), mx_kscale(CIN)
    inp = {}
    inp["h_attn"] = bf(np.maximum(np.random.standard_normal((B, P, N)), 0.0) * s[None, :, None])
    inp["x"] = bf(np.random.standard_normal((B, CIN, N)) * t[None, :, None])
    conv3_w = np.random.standard_normal((COUT, P)) * 1.5 / np.sqrt(P) / s[None, :]
    inp["conv3_w_words"], inp["conv3_w_scales"] = pack4(conv3_w.T)
    inp["bn3_g"] = bf(np.random.uniform(0.5, 1.5, COUT))
    inp["bn3_b"] = bf(np.random.standard_normal(COUT) * 0.3)
    inp["bn3_m"] = bf(np.random.standard_normal(COUT) * 0.3)
    inp["bn3_v"] = bf(np.random.uniform(0.5, 1.5, COUT))
    sc_w = np.random.standard_normal((COUT, CIN)) / np.sqrt(CIN) / t[None, :]
    inp["sc_w_words"], inp["sc_w_scales"] = pack4(sc_w.T)
    inp["sc_b"] = bf(np.random.standard_normal(COUT) * 0.3)
    inp["scbn_g"] = bf(np.random.uniform(0.5, 1.5, COUT))
    inp["scbn_b"] = bf(np.random.standard_normal(COUT) * 0.3)
    inp["scbn_m"] = bf(np.random.standard_normal(COUT) * 0.3)
    inp["scbn_v"] = bf(np.random.uniform(0.5, 1.5, COUT))
    return inp


def reference(h_attn, x, conv3_w_words, conv3_w_scales, bn3_g, bn3_b, bn3_m, bn3_v, sc_w_words, sc_w_scales, sc_b, scbn_g, scbn_b, scbn_m, scbn_v):
    main = bn(unpack4(conv3_w_words, conv3_w_scales).T @ mxq(f64(h_attn), 1, "e5m2"), bn3_g, bn3_b, bn3_m, bn3_v)
    short = (unpack4(sc_w_words, sc_w_scales).T @ mxq(f64(x), 1, "e5m2")) + f64(sc_b)[None, :, None]
    short = bn(short, scbn_g, scbn_b, scbn_m, scbn_v)
    return np.maximum(main + short, 0.0)

@@ -1,0 +1,233 @@
+from contextlib import ExitStack
+
+import concourse.mybir as mybir
+from concourse.masks import make_identity
+
+B, CIN, CMID, COUT, NPOS = 2, 1024, 512, 2048, 512
+EPS = 1e-5
+FLOPS = 2 * B * COUT * NPOS * (CIN + CMID)
+
+F32 = mybir.dt.float32
+BF16 = mybir.dt.bfloat16
+I32 = mybir.dt.int32
+U32 = mybir.dt.uint32
+U8 = mybir.dt.uint8
+E5M2X4 = mybir.dt.float8_e5m2_x4
+E2M1X4 = mybir.dt.float4_e2m1fn_x4
+ALU = mybir.AluOpType
+ACT = mybir.ActivationFunctionType
+
+P = 128
+PACK = 4
+K_PASS = P * PACK
+CT = COUT // P
+TILES = B * CT
+BANKS = 8
+HEAD_CT = 4
+EARLY_MAINS = 12
+F32_MAX = 3.4028234663852886e38
+
+
+def tile_bottleneck_transformer_pb_kernel(
+    tc, h_attn, x, conv3_w_words, conv3_w_scales, bn3_g, bn3_b, bn3_m, bn3_v,
+    sc_w_words, sc_w_scales, sc_b, scbn_g, scbn_b, scbn_m, scbn_v, out,
+):
+    nc = tc.nc
+    with ExitStack() as ctx:
+        keep = ctx.enter_context(tc.tile_pool(name="keep", bufs=1))
+        psum = ctx.enter_context(tc.psum_pool(name="psum", bufs=1))
+        ctx.enter_context(tc.manual_schedule())
+
+        raw = [keep.tile([P, PACK, NPOS], BF16, name="raw%d" % u, align_bytes=64) for u in range(3 * B)]
+        grouped = [keep.tile([P, NPOS, PACK], BF16, name="grouped%d" % u, align_bytes=64) for u in range(3 * B)]
+        codes = [keep.tile([P, NPOS], U32, name="codes%d" % u, align_bytes=64) for u in range(3 * B)]
+        scales = [keep.tile([P, NPOS], U8, name="scales%d" % u, align_bytes=64) for u in range(3 * B)]
+        w_main = keep.tile([P, 2 * COUT], U8, align_bytes=64)
+        w_short_head = keep.tile([P, 2, 2 * P * HEAD_CT], U8, align_bytes=64)
+        w_short_rest = keep.tile([P, 2, 2 * P * (CT - HEAD_CT)], U8, align_bytes=64)
+        plane_main = keep.tile([P, COUT], U8, align_bytes=64)
+        plane_short = keep.tile([P, 2, COUT], U8, align_bytes=64)
+        rows = keep.tile([P, 2, P], BF16, align_bytes=64)
+        ident = keep.tile([P, P], BF16, align_bytes=64)
+        std = keep.tile([P, 2 * CT], F32)
+        inv = keep.tile([P, 2 * CT], F32)
+        terms = keep.tile([P, 7 * CT], F32)
+        gain = keep.tile([P, 2 * CT], F32)
+        parts = keep.tile([P, 3, CT], F32)
+        shift = keep.tile([P, CT], F32)
+        res = [keep.tile([P, NPOS], F32, name="res%d" % n, align_bytes=64) for n in range(TILES)]
+
+        def load_operand(u):
+            b, s = divmod(u, 3)
+            src = h_attn[b] if s == 0 else x[b, (s - 1) * K_PASS : s * K_PASS, :]
+            nc.sync.dma_start(out=raw[u][:], in_=src.rearrange("(p j) n -> p j n", j=PACK))
+
+        def load_vector(eng, slot, place, vec):
+            eng.dma_start(out=rows[CT * place : CT * (place + 1), slot, :], in_=vec.rearrange("(i p) -> i p", p=P))
+
+        def interleave(copy, u, c0, c1):
+            copy(
+                out=grouped[u][:, c0:c1, :].rearrange("p (c i) t -> p c t i", i=4),
+                in_=raw[u][:, :, c0:c1].rearrange("p t (c i) -> p c t i", i=4),
+            )
+
+        def quantize(u):
+            nc.vector.quantize_mx(
+                out=codes[u][:].bitcast(E5M2X4),
+                scales=scales[u][:],
+                in_=grouped[u][:].rearrange("p n t -> p (n t)"),
+            )
+
+        def bank_tile(bank):
+            return psum.tile([P, NPOS], F32, name="acc", tag="bank%d" % bank)
+
+        def main_product(n, bank):
+            b, i = divmod(n, CT)
+            acc = bank_tile(bank)
+            nc.tensor.matmul_mx(
+                out=acc[:],
+                lhsT=w_main[:, 2 * P * i : 2 * P * (i + 1)].bitcast(E2M1X4),
+                lhsT_scale=plane_main[:, P * i : P * (i + 1)],
+                rhs=codes[3 * b][:].bitcast(E5M2X4),
+                rhs_scale=scales[3 * b][:],
+                start=True,
+                stop=True,
+            )
+            return acc
+
+        def main_out(n, acc):
+            i = n % CT
+            nc.scalar.activation(out=res[n][:], in_=acc[:], func=ACT.Identity, scale=gain[:, i : i + 1], bias=shift[:, i : i + 1])
+
+        def short_product(n, bank):
+            b, i = divmod(n, CT)
+            acc = bank_tile(bank)
+            words, j = (w_short_head, i) if i < HEAD_CT else (w_short_rest, i - HEAD_CT)
+            for g in range(2):
+                nc.tensor.matmul_mx(
+                    out=acc[:],
+                    lhsT=words[:, g, 2 * P * j : 2 * P * (j + 1)].bitcast(E2M1X4),
+                    lhsT_scale=plane_short[:, g, P * i : P * (i + 1)],
+                    rhs=codes[3 * b + 1 + g][:].bitcast(E5M2X4),
+                    rhs_scale=scales[3 * b + 1 + g][:],
+                    start=(g == 0),
+                    stop=(g == 1),
+                )
+            nc.vector.scalar_tensor_tensor(
+                out=res[n][:], in0=acc[:], scalar=gain[:, CT + i : CT + i + 1], in1=res[n][:],
+                op0=ALU.mult, op1=ALU.add,
+            )
+
+        def finish(n):
+            b, i = divmod(n, CT)
+            if n in (18, 21, 24, 27, 29, 30):
+                nc.scalar.activation(out=res[n][:], in_=res[n][:], func=ACT.Relu)
+            elif n == TILES - 1:
+                nc.vector.tensor_scalar(out=res[n][:], in0=res[n][:], scalar1=0.0, scalar2=None, op0=ALU.max)
+            else:
+                nc.gpsimd.tensor_scalar(
+                    out=res[n][:], in0=res[n][:], scalar1=F32_MAX, scalar2=0.0, op0=ALU.min, op1=ALU.max
+                )
+            nc.sync.dma_start(out=out[b, P * i : P * (i + 1), :], in_=res[n][:])
+
+        nc.vector.memset(rows[:].rearrange("p s r -> p (s r)").bitcast(I32), 0)
+        nc.vector.memset(plane_main[:].bitcast(I32), 0)
+        nc.vector.memset(plane_short[:].rearrange("p g n -> p (g n)").bitcast(I32), 0)
+        make_identity(nc, ident[:])
+
+        load_operand(0)
+        nc.sync.dma_start(out=w_main[:].bitcast(I32), in_=conv3_w_words[0].bitcast(I32))
+        load_vector(nc.scalar, 0, 0, bn3_v)
+        load_vector(nc.scalar, 0, 1, scbn_v)
+        for place, vec in enumerate((bn3_g, scbn_g, bn3_m, scbn_m, bn3_b)):
+            load_vector(nc.scalar, 1, place, vec)
+        load_vector(nc.gpsimd, 1, 5, scbn_b)
+        load_vector(nc.gpsimd, 1, 6, sc_b)
+        for q in range(4):
+            nc.sync.dma_start(
+                out=plane_main[32 * q : 32 * q + 4, :].bitcast(I32),
+                in_=conv3_w_scales[0, 4 * q : 4 * q + 4, :].bitcast(I32),
+            )
+        load_operand(1)
+        load_operand(2)
+        head_bytes = 2 * P * HEAD_CT
+        nc.sync.dma_start(
+            out=w_short_head[:].bitcast(I32),
+            in_=sc_w_words[:, :, :head_bytes].rearrange("g p n -> p g n").bitcast(I32),
+        )
+        for q in range(4):
+            nc.sync.dma_start(
+                out=plane_short[32 * q : 32 * q + 4, :, :].bitcast(I32),
+                in_=sc_w_scales[:, 4 * q : 4 * q + 4, :].rearrange("g r n -> r g n").bitcast(I32),
+            )
+        nc.sync.dma_start(
+            out=w_short_rest[:].bitcast(I32),
+            in_=sc_w_words[:, :, head_bytes:].rearrange("g p n -> p g n").bitcast(I32),
+        )
+        for u in (3, 4, 5):
+            load_operand(u)
+
+        cols_var = psum.tile([P, P], BF16, name="cols_var", tag="bank6")
+        cols_rest = psum.tile([P, P], BF16, name="cols_rest", tag="bank7")
+        nc.tensor.transpose(cols_var[:], rows[:, 0, :], ident[:])
+        nc.tensor.transpose(cols_rest[:], rows[:, 1, :], ident[:])
+        nc.scalar.activation(out=std[:], in_=cols_var[:, : 2 * CT], func=ACT.Sqrt, bias=EPS)
+
+        half = NPOS // 2
+        quarter = NPOS // 4
+        interleave(nc.vector.tensor_copy, 0, 0, NPOS)
+        nc.vector.reciprocal(out=inv[:], in_=std[:])
+        quantize(0)
+        nc.vector.tensor_copy(out=terms[:], in_=cols_rest[:, : 7 * CT])
+        interleave(nc.scalar.copy, 1, half, NPOS)
+        interleave(nc.vector.tensor_copy, 1, 0, quarter)
+        nc.vector.tensor_tensor(out=gain[:], in0=terms[:, : 2 * CT], in1=inv[:], op=ALU.mult)
+        nc.vector.tensor_tensor(
+            out=terms[:, 3 * CT : 4 * CT], in0=terms[:, 3 * CT : 4 * CT], in1=terms[:, 6 * CT :], op=ALU.subtract
+        )
+        nc.vector.tensor_tensor(
+            out=parts[:, 2, :], in0=terms[:, 4 * CT : 5 * CT], in1=terms[:, 5 * CT : 6 * CT], op=ALU.add
+        )
+        nc.vector.scalar_tensor_tensor(
+            out=parts[:, :2, :].rearrange("p s i -> p (s i)"), in0=terms[:, 2 * CT : 4 * CT], scalar=-1.0,
+            in1=gain[:], op0=ALU.mult, op1=ALU.mult,
+        )
+        interleave(nc.vector.tensor_copy, 1, quarter, half)
+        nc.vector.tensor_reduce(
+            out=shift[:], in_=parts[:].rearrange("p s i -> p i s"), axis=mybir.AxisListType.X, op=ALU.add
+        )
+        interleave(nc.vector.tensor_copy, 2, 0, half)
+        quantize(1)
+        interleave(nc.vector.tensor_copy, 2, half, NPOS)
+        quantize(2)
+
+        for n in range(EARLY_MAINS):
+            main_out(n, main_product(n, n % BANKS))
+
+        bank = EARLY_MAINS % BANKS
+        m = EARLY_MAINS
+        for n in range(TILES):
+            short_product(n, bank)
+            bank = (bank + 1) % BANKS
+            finish(n)
+            if m < TILES and 3 * (m - EARLY_MAINS) // 2 == n:
+                main_out(m, main_product(m, bank))
+                bank = (bank + 1) % BANKS
+                piece = m - EARLY_MAINS
+                if piece < 4:
+                    interleave(nc.scalar.copy, 4, quarter * piece, quarter * (piece + 1))
+                elif piece < 6:
+                    interleave(nc.scalar.copy, 5, quarter * (piece - 2), quarter * (piece - 1))
+                m += 1
+            if n == 1:
+                interleave(nc.vector.tensor_copy, 3, 0, half)
+            elif n == 2:
+                interleave(nc.vector.tensor_copy, 3, half, NPOS)
+            elif n == 3:
+                quantize(3)
+            elif n == 8:
+                interleave(nc.vector.tensor_copy, 5, 0, half)
+            elif n == 10:
+                quantize(4)
+            elif n == 12:
+                quantize(5)

@@ -25,6 +25,7 @@ TILES = B * CT
 BANKS = 8
 HEAD_CT = 4
 EARLY_MAINS = 12
+PAIRED = 24
 F32_MAX = 3.4028234663852886e38
 
 
@@ -39,10 +40,10 @@ def tile_bottleneck_transformer_pb_kernel(
         ctx.enter_context(tc.manual_schedule())
 
         raw = [keep.tile([P, PACK, NPOS], BF16, name="raw%d" % u, align_bytes=64) for u in range(3 * B)]
-        grouped = [keep.tile([P, NPOS, PACK], BF16, name="grouped%d" % u, align_bytes=64) for u in range(3 * B)]
-        codes = [keep.tile([P, NPOS], U32, name="codes%d" % u, align_bytes=64) for u in range(3 * B)]
-        scales = [keep.tile([P, NPOS], U8, name="scales%d" % u, align_bytes=64) for u in range(3 * B)]
-        w_main = keep.tile([P, 2 * COUT], U8, align_bytes=64)
+        grouped = [keep.tile([P, 3, NPOS, PACK], BF16, name="grouped%d" % b, align_bytes=64) for b in range(B)]
+        codes = [keep.tile([P, 3, NPOS], U32, name="codes%d" % b, align_bytes=64) for b in range(B)]
+        scales = [keep.tile([P, 3, NPOS], U8, name="scales%d" % b, align_bytes=64) for b in range(B)]
+        w_main = [keep.tile([P, COUT], U8, name="w_main%d" % h, align_bytes=64) for h in range(2)]
         w_short_head = keep.tile([P, 2, 2 * P * HEAD_CT], U8, align_bytes=64)
         w_short_rest = keep.tile([P, 2, 2 * P * (CT - HEAD_CT)], U8, align_bytes=64)
         plane_main = keep.tile([P, COUT], U8, align_bytes=64)
@@ -51,11 +52,10 @@ def tile_bottleneck_transformer_pb_kernel(
         ident = keep.tile([P, P], BF16, align_bytes=64)
         std = keep.tile([P, 2 * CT], F32)
         inv = keep.tile([P, 2 * CT], F32)
-        terms = keep.tile([P, 7 * CT], F32)
         gain = keep.tile([P, 2 * CT], F32)
-        parts = keep.tile([P, 3, CT], F32)
+        parts = keep.tile([P, 5, CT], F32)
         shift = keep.tile([P, CT], F32)
-        res = [keep.tile([P, NPOS], F32, name="res%d" % n, align_bytes=64) for n in range(TILES)]
+        res = keep.tile([P, TILES, NPOS], F32, align_bytes=64)
 
         def load_operand(u):
             b, s = divmod(u, 3)
@@ -67,15 +67,15 @@ def tile_bottleneck_transformer_pb_kernel(
 
         def interleave(copy, u, c0, c1):
             copy(
-                out=grouped[u][:, c0:c1, :].rearrange("p (c i) t -> p c t i", i=4),
+                out=grouped[u // 3][:, u % 3, c0:c1, :].rearrange("p (c i) t -> p c t i", i=4),
                 in_=raw[u][:, :, c0:c1].rearrange("p t (c i) -> p c t i", i=4),
             )
 
-        def quantize(u):
+        def quantize(b, s0, s1):
             nc.vector.quantize_mx(
-                out=codes[u][:].bitcast(E5M2X4),
-                scales=scales[u][:],
-                in_=grouped[u][:].rearrange("p n t -> p (n t)"),
+                out=codes[b][:, s0:s1, :].rearrange("p s n -> p (s n)").bitcast(E5M2X4),
+                scales=scales[b][:, s0:s1, :].rearrange("p s n -> p (s n)"),
+                in_=grouped[b][:, s0:s1, :, :].rearrange("p s n t -> p (s n t)"),
             )
 
         def bank_tile(bank):
@@ -86,10 +86,10 @@ def tile_bottleneck_transformer_pb_kernel(
             acc = bank_tile(bank)
             nc.tensor.matmul_mx(
                 out=acc[:],
-                lhsT=w_main[:, 2 * P * i : 2 * P * (i + 1)].bitcast(E2M1X4),
+                lhsT=w_main[i // 8][:, 2 * P * (i % 8) : 2 * P * (i % 8 + 1)].bitcast(E2M1X4),
                 lhsT_scale=plane_main[:, P * i : P * (i + 1)],
-                rhs=codes[3 * b][:].bitcast(E5M2X4),
-                rhs_scale=scales[3 * b][:],
+                rhs=codes[b][:, 0, :].bitcast(E5M2X4),
+                rhs_scale=scales[b][:, 0, :],
                 start=True,
                 stop=True,
             )
@@ -97,7 +97,7 @@ def tile_bottleneck_transformer_pb_kernel(
 
         def main_out(n, acc):
             i = n % CT
-            nc.scalar.activation(out=res[n][:], in_=acc[:], func=ACT.Identity, scale=gain[:, i : i + 1], bias=shift[:, i : i + 1])
+            nc.scalar.activation(out=res[:, n, :], in_=acc[:], func=ACT.Identity, scale=gain[:, i : i + 1], bias=shift[:, i : i + 1])
 
         def short_product(n, bank):
             b, i = divmod(n, CT)
@@ -108,48 +108,52 @@ def tile_bottleneck_transformer_pb_kernel(
                     out=acc[:],
                     lhsT=words[:, g, 2 * P * j : 2 * P * (j + 1)].bitcast(E2M1X4),
                     lhsT_scale=plane_short[:, g, P * i : P * (i + 1)],
-                    rhs=codes[3 * b + 1 + g][:].bitcast(E5M2X4),
-                    rhs_scale=scales[3 * b + 1 + g][:],
+                    rhs=codes[b][:, 1 + g, :].bitcast(E5M2X4),
+                    rhs_scale=scales[b][:, 1 + g, :],
                     start=(g == 0),
                     stop=(g == 1),
                 )
             nc.vector.scalar_tensor_tensor(
-                out=res[n][:], in0=acc[:], scalar=gain[:, CT + i : CT + i + 1], in1=res[n][:],
+                out=res[:, n, :], in0=acc[:], scalar=gain[:, CT + i : CT + i + 1], in1=res[:, n, :],
                 op0=ALU.mult, op1=ALU.add,
             )
 
-        def finish(n):
+        def finish(n, count, engine):
             b, i = divmod(n, CT)
-            if n in (18, 21, 24, 27, 29, 30):
-                nc.scalar.activation(out=res[n][:], in_=res[n][:], func=ACT.Relu)
-            elif n == TILES - 1:
-                nc.vector.tensor_scalar(out=res[n][:], in0=res[n][:], scalar1=0.0, scalar2=None, op0=ALU.max)
+            vals = res[:, n : n + count, :].rearrange("p t n -> p (t n)")
+            if engine == "scalar":
+                nc.scalar.activation(out=vals, in_=vals, func=ACT.Relu)
+            elif engine == "vector":
+                nc.vector.tensor_scalar(out=vals, in0=vals, scalar1=0.0, scalar2=None, op0=ALU.max)
             else:
-                nc.gpsimd.tensor_scalar(
-                    out=res[n][:], in0=res[n][:], scalar1=F32_MAX, scalar2=0.0, op0=ALU.min, op1=ALU.max
-                )
-            nc.sync.dma_start(out=out[b, P * i : P * (i + 1), :], in_=res[n][:])
+                nc.gpsimd.tensor_scalar(out=vals, in0=vals, scalar1=F32_MAX, scalar2=0.0, op0=ALU.min, op1=ALU.max)
+            nc.sync.dma_start(
+                out=out[b, P * i : P * (i + count), :].rearrange("(t p) n -> p t n", p=P),
+                in_=res[:, n : n + count, :],
+            )
 
-        nc.vector.memset(rows[:].rearrange("p s r -> p (s r)").bitcast(I32), 0)
+        nc.vector.memset(rows[96:, 0, :].bitcast(I32), 0)
+        nc.vector.memset(rows[32:64, 1, :].bitcast(I32), 0)
+        nc.vector.memset(rows[64:, 1, :].bitcast(I32), 0)
         nc.vector.memset(plane_main[:].bitcast(I32), 0)
         nc.vector.memset(plane_short[:].rearrange("p g n -> p (g n)").bitcast(I32), 0)
         make_identity(nc, ident[:])
 
         load_operand(0)
-        nc.sync.dma_start(out=w_main[:].bitcast(I32), in_=conv3_w_words[0].bitcast(I32))
-        load_vector(nc.scalar, 0, 0, bn3_v)
-        load_vector(nc.scalar, 0, 1, scbn_v)
-        for place, vec in enumerate((bn3_g, scbn_g, bn3_m, scbn_m, bn3_b)):
-            load_vector(nc.scalar, 1, place, vec)
-        load_vector(nc.gpsimd, 1, 5, scbn_b)
-        load_vector(nc.gpsimd, 1, 6, sc_b)
+        for place, vec in enumerate((bn3_v, scbn_v, bn3_g, scbn_g, bn3_m, scbn_m)):
+            load_vector(nc.sync, 0, place, vec)
+        load_operand(1)
+        load_vector(nc.gpsimd, 1, 1, scbn_b)
+        load_vector(nc.gpsimd, 1, 2, sc_b)
         for q in range(4):
             nc.sync.dma_start(
                 out=plane_main[32 * q : 32 * q + 4, :].bitcast(I32),
                 in_=conv3_w_scales[0, 4 * q : 4 * q + 4, :].bitcast(I32),
             )
-        load_operand(1)
+        load_vector(nc.sync, 1, 0, bn3_b)
+        nc.sync.dma_start(out=w_main[0][:].bitcast(I32), in_=conv3_w_words[0, :, :COUT].bitcast(I32))
         load_operand(2)
+        nc.sync.dma_start(out=w_main[1][:].bitcast(I32), in_=conv3_w_words[0, :, COUT:].bitcast(I32))
         head_bytes = 2 * P * HEAD_CT
         nc.sync.dma_start(
             out=w_short_head[:].bitcast(I32),
@@ -160,46 +164,42 @@ def tile_bottleneck_transformer_pb_kernel(
                 out=plane_short[32 * q : 32 * q + 4, :, :].bitcast(I32),
                 in_=sc_w_scales[:, 4 * q : 4 * q + 4, :].rearrange("g r n -> r g n").bitcast(I32),
             )
+        load_operand(3)
         nc.sync.dma_start(
             out=w_short_rest[:].bitcast(I32),
             in_=sc_w_words[:, :, head_bytes:].rearrange("g p n -> p g n").bitcast(I32),
         )
-        for u in (3, 4, 5):
-            load_operand(u)
+        load_operand(4)
+        load_operand(5)
 
-        cols_var = psum.tile([P, P], BF16, name="cols_var", tag="bank6")
-        cols_rest = psum.tile([P, P], BF16, name="cols_rest", tag="bank7")
-        nc.tensor.transpose(cols_var[:], rows[:, 0, :], ident[:])
-        nc.tensor.transpose(cols_rest[:], rows[:, 1, :], ident[:])
-        nc.scalar.activation(out=std[:], in_=cols_var[:, : 2 * CT], func=ACT.Sqrt, bias=EPS)
+        cols_early = psum.tile([P, P], BF16, name="cols_early", tag="bank6")
+        cols_late = psum.tile([P, P], BF16, name="cols_late", tag="bank7")
+        nc.tensor.transpose(cols_early[:], rows[:, 0, :], ident[:])
+        nc.tensor.transpose(cols_late[:], rows[:, 1, :], ident[:])
+        nc.scalar.activation(out=std[:], in_=cols_early[:, : 2 * CT], func=ACT.Sqrt, bias=EPS)
 
         half = NPOS // 2
         quarter = NPOS // 4
-        interleave(nc.vector.tensor_copy, 0, 0, NPOS)
+        interleave(nc.vector.tensor_copy, 0, 0, 3 * quarter)
+        interleave(nc.scalar.copy, 0, 3 * quarter, NPOS)
         nc.vector.reciprocal(out=inv[:], in_=std[:])
-        quantize(0)
-        nc.vector.tensor_copy(out=terms[:], in_=cols_rest[:, : 7 * CT])
+        quantize(0, 0, 1)
         interleave(nc.scalar.copy, 1, half, NPOS)
-        interleave(nc.vector.tensor_copy, 1, 0, quarter)
-        nc.vector.tensor_tensor(out=gain[:], in0=terms[:, : 2 * CT], in1=inv[:], op=ALU.mult)
-        nc.vector.tensor_tensor(
-            out=terms[:, 3 * CT : 4 * CT], in0=terms[:, 3 * CT : 4 * CT], in1=terms[:, 6 * CT :], op=ALU.subtract
-        )
-        nc.vector.tensor_tensor(
-            out=parts[:, 2, :], in0=terms[:, 4 * CT : 5 * CT], in1=terms[:, 5 * CT : 6 * CT], op=ALU.add
-        )
+        nc.vector.tensor_tensor(out=gain[:], in0=cols_early[:, 2 * CT : 4 * CT], in1=inv[:], op=ALU.mult)
+        interleave(nc.vector.tensor_copy, 1, 0, half)
         nc.vector.scalar_tensor_tensor(
-            out=parts[:, :2, :].rearrange("p s i -> p (s i)"), in0=terms[:, 2 * CT : 4 * CT], scalar=-1.0,
+            out=parts[:, :2, :].rearrange("p s i -> p (s i)"), in0=cols_early[:, 4 * CT : 6 * CT], scalar=-1.0,
             in1=gain[:], op0=ALU.mult, op1=ALU.mult,
         )
-        interleave(nc.vector.tensor_copy, 1, quarter, half)
+        nc.vector.tensor_tensor(out=parts[:, 2, :], in0=cols_late[:, 2 * CT : 3 * CT], in1=gain[:, CT:], op=ALU.mult)
+        nc.vector.tensor_copy(out=parts[:, 3:, :].rearrange("p s i -> p (s i)"), in_=cols_late[:, : 2 * CT])
         nc.vector.tensor_reduce(
             out=shift[:], in_=parts[:].rearrange("p s i -> p i s"), axis=mybir.AxisListType.X, op=ALU.add
         )
-        interleave(nc.vector.tensor_copy, 2, 0, half)
-        quantize(1)
-        interleave(nc.vector.tensor_copy, 2, half, NPOS)
-        quantize(2)
+        quantize(0, 1, 2)
+        interleave(nc.vector.tensor_copy, 2, 0, NPOS)
+        quantize(0, 2, 3)
+        interleave(nc.vector.tensor_copy, 3, 0, NPOS)
 
         for n in range(EARLY_MAINS):
             main_out(n, main_product(n, n % BANKS))
@@ -209,25 +209,23 @@ def tile_bottleneck_transformer_pb_kernel(
         for n in range(TILES):
             short_product(n, bank)
             bank = (bank + 1) % BANKS
-            finish(n)
+            if n < PAIRED:
+                if n % 2 == 1:
+                    finish(n - 1, 2, "gpsimd")
+            elif n == TILES - 1:
+                finish(n, 1, "vector")
+            else:
+                finish(n, 1, "gpsimd" if n % 2 == 0 and n < TILES - 2 else "scalar")
             if m < TILES and 3 * (m - EARLY_MAINS) // 2 == n:
                 main_out(m, main_product(m, bank))
                 bank = (bank + 1) % BANKS
                 piece = m - EARLY_MAINS
                 if piece < 4:
                     interleave(nc.scalar.copy, 4, quarter * piece, quarter * (piece + 1))
-                elif piece < 6:
-                    interleave(nc.scalar.copy, 5, quarter * (piece - 2), quarter * (piece - 1))
                 m += 1
-            if n == 1:
-                interleave(nc.vector.tensor_copy, 3, 0, half)
-            elif n == 2:
-                interleave(nc.vector.tensor_copy, 3, half, NPOS)
-            elif n == 3:
-                quantize(3)
-            elif n == 8:
-                interleave(nc.vector.tensor_copy, 5, 0, half)
-            elif n == 10:
-                quantize(4)
-            elif n == 12:
-                quantize(5)
+            if n == 0:
+                quantize(1, 0, 1)
+            elif n == 5:
+                interleave(nc.vector.tensor_copy, 5, 0, NPOS)
+            elif n == 9:
+                quantize(1, 1, 3)

@@ -23,7 +23,7 @@ K_PASS = P * PACK
 CT = COUT // P
 TILES = B * CT
 BANKS = 8
-HEAD_CT = 4
+HEAD_CT = 5
 EARLY_MAINS = 12
 PAIRED = 24
 F32_MAX = 3.4028234663852886e38
@@ -47,7 +47,8 @@ def tile_bottleneck_transformer_pb_kernel(
         w_short_head = keep.tile([P, 2, 2 * P * HEAD_CT], U8, align_bytes=64)
         w_short_rest = keep.tile([P, 2, 2 * P * (CT - HEAD_CT)], U8, align_bytes=64)
         plane_main = keep.tile([P, COUT], U8, align_bytes=64)
-        plane_short = keep.tile([P, 2, COUT], U8, align_bytes=64)
+        plane_short_head = keep.tile([P, 2, P * HEAD_CT], U8, align_bytes=64)
+        plane_short_rest = keep.tile([P, 2, P * (CT - HEAD_CT)], U8, align_bytes=64)
         rows = keep.tile([P, 2, P], BF16, align_bytes=64)
         ident = keep.tile([P, P], BF16, align_bytes=64)
         std = keep.tile([P, 2 * CT], F32)
@@ -102,12 +103,15 @@ def tile_bottleneck_transformer_pb_kernel(
         def short_product(n, bank):
             b, i = divmod(n, CT)
             acc = bank_tile(bank)
-            words, j = (w_short_head, i) if i < HEAD_CT else (w_short_rest, i - HEAD_CT)
+            if i < HEAD_CT:
+                words, plane, j = w_short_head, plane_short_head, i
+            else:
+                words, plane, j = w_short_rest, plane_short_rest, i - HEAD_CT
             for g in range(2):
                 nc.tensor.matmul_mx(
                     out=acc[:],
                     lhsT=words[:, g, 2 * P * j : 2 * P * (j + 1)].bitcast(E2M1X4),
-                    lhsT_scale=plane_short[:, g, P * i : P * (i + 1)],
+                    lhsT_scale=plane[:, g, P * j : P * (j + 1)],
                     rhs=codes[b][:, 1 + g, :].bitcast(E5M2X4),
                     rhs_scale=scales[b][:, 1 + g, :],
                     start=(g == 0),
@@ -136,7 +140,8 @@ def tile_bottleneck_transformer_pb_kernel(
         nc.vector.memset(rows[32:64, 1, :].bitcast(I32), 0)
         nc.vector.memset(rows[64:, 1, :].bitcast(I32), 0)
         nc.vector.memset(plane_main[:].bitcast(I32), 0)
-        nc.vector.memset(plane_short[:].rearrange("p g n -> p (g n)").bitcast(I32), 0)
+        nc.vector.memset(plane_short_head[:].rearrange("p g n -> p (g n)").bitcast(I32), 0)
+        nc.vector.memset(plane_short_rest[:].rearrange("p g n -> p (g n)").bitcast(I32), 0)
         make_identity(nc, ident[:])
 
         load_operand(0)
@@ -145,30 +150,28 @@ def tile_bottleneck_transformer_pb_kernel(
         load_operand(1)
         load_vector(nc.gpsimd, 1, 1, scbn_b)
         load_vector(nc.gpsimd, 1, 2, sc_b)
-        for q in range(4):
+        for r in range(4):
             nc.sync.dma_start(
-                out=plane_main[32 * q : 32 * q + 4, :].bitcast(I32),
-                in_=conv3_w_scales[0, 4 * q : 4 * q + 4, :].bitcast(I32),
+                out=plane_main[r:P:32, :].bitcast(I32), in_=conv3_w_scales[0, r:16:4, :].bitcast(I32)
             )
         load_vector(nc.sync, 1, 0, bn3_b)
         nc.sync.dma_start(out=w_main[0][:].bitcast(I32), in_=conv3_w_words[0, :, :COUT].bitcast(I32))
         load_operand(2)
         nc.sync.dma_start(out=w_main[1][:].bitcast(I32), in_=conv3_w_words[0, :, COUT:].bitcast(I32))
-        head_bytes = 2 * P * HEAD_CT
-        nc.sync.dma_start(
-            out=w_short_head[:].bitcast(I32),
-            in_=sc_w_words[:, :, :head_bytes].rearrange("g p n -> p g n").bitcast(I32),
-        )
-        for q in range(4):
-            nc.sync.dma_start(
-                out=plane_short[32 * q : 32 * q + 4, :, :].bitcast(I32),
-                in_=sc_w_scales[:, 4 * q : 4 * q + 4, :].rearrange("g r n -> r g n").bitcast(I32),
-            )
         load_operand(3)
-        nc.sync.dma_start(
-            out=w_short_rest[:].bitcast(I32),
-            in_=sc_w_words[:, :, head_bytes:].rearrange("g p n -> p g n").bitcast(I32),
-        )
+        for words, plane, c0, c1 in (
+            (w_short_head, plane_short_head, 0, P * HEAD_CT),
+            (w_short_rest, plane_short_rest, P * HEAD_CT, COUT),
+        ):
+            nc.sync.dma_start(
+                out=words[:].bitcast(I32),
+                in_=sc_w_words[:, :, 2 * c0 : 2 * c1].rearrange("g p n -> p g n").bitcast(I32),
+            )
+            for r in range(4):
+                nc.sync.dma_start(
+                    out=plane[r:P:32, :, :].bitcast(I32),
+                    in_=sc_w_scales[:, r:16:4, c0:c1].rearrange("g q n -> q g n").bitcast(I32),
+                )
         load_operand(4)
         load_operand(5)
 
@@ -211,7 +214,7 @@ def tile_bottleneck_transformer_pb_kernel(
             bank = (bank + 1) % BANKS
             if n < PAIRED:
                 if n % 2 == 1:
-                    finish(n - 1, 2, "gpsimd")
+                    finish(n - 1, 2, "scalar" if n in (17, 21) else "gpsimd")
             elif n == TILES - 1:
                 finish(n, 1, "vector")
             else:

@@ -23,10 +23,16 @@ K_PASS = P * PACK
 CT = COUT // P
 TILES = B * CT
 BANKS = 8
+OPERANDS = 3
+HALF = NPOS // 2
+QUARTER = NPOS // 4
+F32_MAX = 3.4028234663852886e38
+
 HEAD_CT = 5
 EARLY_MAINS = 12
-PAIRED = 24
-F32_MAX = 3.4028234663852886e38
+PAIRED = 6
+COPY_AT = 5
+QUANTIZE_AT = 11
 
 
 def tile_bottleneck_transformer_pb_kernel(
@@ -39,10 +45,12 @@ def tile_bottleneck_transformer_pb_kernel(
         psum = ctx.enter_context(tc.psum_pool(name="psum", bufs=1))
         ctx.enter_context(tc.manual_schedule())
 
-        raw = [keep.tile([P, PACK, NPOS], BF16, name="raw%d" % u, align_bytes=64) for u in range(3 * B)]
-        grouped = [keep.tile([P, 3, NPOS, PACK], BF16, name="grouped%d" % b, align_bytes=64) for b in range(B)]
-        codes = [keep.tile([P, 3, NPOS], U32, name="codes%d" % b, align_bytes=64) for b in range(B)]
-        scales = [keep.tile([P, 3, NPOS], U8, name="scales%d" % b, align_bytes=64) for b in range(B)]
+        raw = [keep.tile([P, PACK, NPOS], BF16, name="raw%d" % u, align_bytes=64) for u in range(OPERANDS * B)]
+        grouped = [
+            keep.tile([P, OPERANDS, NPOS, PACK], BF16, name="grouped%d" % b, align_bytes=64) for b in range(B)
+        ]
+        codes = [keep.tile([P, OPERANDS, NPOS], U32, name="codes%d" % b, align_bytes=64) for b in range(B)]
+        scales = [keep.tile([P, OPERANDS, NPOS], U8, name="scales%d" % b, align_bytes=64) for b in range(B)]
         w_main = [keep.tile([P, COUT], U8, name="w_main%d" % h, align_bytes=64) for h in range(2)]
         w_short_head = keep.tile([P, 2, 2 * P * HEAD_CT], U8, align_bytes=64)
         w_short_rest = keep.tile([P, 2, 2 * P * (CT - HEAD_CT)], U8, align_bytes=64)
@@ -59,17 +67,17 @@ def tile_bottleneck_transformer_pb_kernel(
         res = keep.tile([P, TILES, NPOS], F32, align_bytes=64)
 
         def load_operand(u):
-            b, s = divmod(u, 3)
+            b, s = divmod(u, OPERANDS)
             src = h_attn[b] if s == 0 else x[b, (s - 1) * K_PASS : s * K_PASS, :]
-            nc.sync.dma_start(out=raw[u][:], in_=src.rearrange("(p j) n -> p j n", j=PACK))
+            nc.sync.dma_start(out=raw[u][:], in_=src.rearrange("(p t) n -> p t n", t=PACK))
 
-        def load_vector(eng, slot, place, vec):
-            eng.dma_start(out=rows[CT * place : CT * (place + 1), slot, :], in_=vec.rearrange("(i p) -> i p", p=P))
+        def load_vector(eng, group, place, vec):
+            eng.dma_start(out=rows[CT * place : CT * (place + 1), group, :], in_=vec.rearrange("(i p) -> i p", p=P))
 
-        def interleave(copy, u, c0, c1):
+        def interleave(copy, u, n0, n1):
             copy(
-                out=grouped[u // 3][:, u % 3, c0:c1, :].rearrange("p (c i) t -> p c t i", i=4),
-                in_=raw[u][:, :, c0:c1].rearrange("p t (c i) -> p c t i", i=4),
+                out=grouped[u // OPERANDS][:, u % OPERANDS, n0:n1, :].rearrange("p (c i) t -> p c t i", i=4),
+                in_=raw[u][:, :, n0:n1].rearrange("p t (c i) -> p c t i", i=4),
             )
 
         def quantize(b, s0, s1):
@@ -79,30 +87,26 @@ def tile_bottleneck_transformer_pb_kernel(
                 in_=grouped[b][:, s0:s1, :, :].rearrange("p s n t -> p (s n t)"),
             )
 
-        def bank_tile(bank):
-            return psum.tile([P, NPOS], F32, name="acc", tag="bank%d" % bank)
-
         def main_product(n, bank):
             b, i = divmod(n, CT)
-            acc = bank_tile(bank)
+            h, j = divmod(i, CT // 2)
+            acc = psum.tile([P, NPOS], F32, name="acc", tag="bank%d" % bank)
             nc.tensor.matmul_mx(
                 out=acc[:],
-                lhsT=w_main[i // 8][:, 2 * P * (i % 8) : 2 * P * (i % 8 + 1)].bitcast(E2M1X4),
+                lhsT=w_main[h][:, 2 * P * j : 2 * P * (j + 1)].bitcast(E2M1X4),
                 lhsT_scale=plane_main[:, P * i : P * (i + 1)],
                 rhs=codes[b][:, 0, :].bitcast(E5M2X4),
                 rhs_scale=scales[b][:, 0, :],
                 start=True,
                 stop=True,
             )
-            return acc
-
-        def main_out(n, acc):
-            i = n % CT
-            nc.scalar.activation(out=res[:, n, :], in_=acc[:], func=ACT.Identity, scale=gain[:, i : i + 1], bias=shift[:, i : i + 1])
+            nc.scalar.activation(
+                out=res[:, n, :], in_=acc[:], func=ACT.Identity, scale=gain[:, i : i + 1], bias=shift[:, i : i + 1]
+            )
 
         def short_product(n, bank):
             b, i = divmod(n, CT)
-            acc = bank_tile(bank)
+            acc = psum.tile([P, NPOS], F32, name="acc", tag="bank%d" % bank)
             if i < HEAD_CT:
                 words, plane, j = w_short_head, plane_short_head, i
             else:
@@ -122,15 +126,18 @@ def tile_bottleneck_transformer_pb_kernel(
                 op0=ALU.mult, op1=ALU.add,
             )
 
-        def finish(n, count, engine):
+        def relu_scalar(vals):
+            nc.scalar.activation(out=vals, in_=vals, func=ACT.Relu)
+
+        def relu_vector(vals):
+            nc.vector.tensor_scalar(out=vals, in0=vals, scalar1=0.0, scalar2=None, op0=ALU.max)
+
+        def relu_gpsimd(vals):
+            nc.gpsimd.tensor_scalar(out=vals, in0=vals, scalar1=F32_MAX, scalar2=0.0, op0=ALU.min, op1=ALU.max)
+
+        def finish(relu, n, count):
             b, i = divmod(n, CT)
-            vals = res[:, n : n + count, :].rearrange("p t n -> p (t n)")
-            if engine == "scalar":
-                nc.scalar.activation(out=vals, in_=vals, func=ACT.Relu)
-            elif engine == "vector":
-                nc.vector.tensor_scalar(out=vals, in0=vals, scalar1=0.0, scalar2=None, op0=ALU.max)
-            else:
-                nc.gpsimd.tensor_scalar(out=vals, in0=vals, scalar1=F32_MAX, scalar2=0.0, op0=ALU.min, op1=ALU.max)
+            relu(res[:, n : n + count, :].rearrange("p t n -> p (t n)"))
             nc.sync.dma_start(
                 out=out[b, P * i : P * (i + count), :].rearrange("(t p) n -> p t n", p=P),
                 in_=res[:, n : n + count, :],
@@ -151,9 +158,7 @@ def tile_bottleneck_transformer_pb_kernel(
         load_vector(nc.gpsimd, 1, 1, scbn_b)
         load_vector(nc.gpsimd, 1, 2, sc_b)
         for r in range(4):
-            nc.sync.dma_start(
-                out=plane_main[r:P:32, :].bitcast(I32), in_=conv3_w_scales[0, r:16:4, :].bitcast(I32)
-            )
+            nc.sync.dma_start(out=plane_main[r:P:32, :].bitcast(I32), in_=conv3_w_scales[0, r:16:4, :].bitcast(I32))
         load_vector(nc.sync, 1, 0, bn3_b)
         nc.sync.dma_start(out=w_main[0][:].bitcast(I32), in_=conv3_w_words[0, :, :COUT].bitcast(I32))
         load_operand(2)
@@ -175,21 +180,19 @@ def tile_bottleneck_transformer_pb_kernel(
         load_operand(4)
         load_operand(5)
 
-        cols_early = psum.tile([P, P], BF16, name="cols_early", tag="bank6")
-        cols_late = psum.tile([P, P], BF16, name="cols_late", tag="bank7")
+        cols_early = psum.tile([P, P], BF16, name="cols_early", tag="bank%d" % (BANKS - 2))
+        cols_late = psum.tile([P, P], BF16, name="cols_late", tag="bank%d" % (BANKS - 1))
         nc.tensor.transpose(cols_early[:], rows[:, 0, :], ident[:])
         nc.tensor.transpose(cols_late[:], rows[:, 1, :], ident[:])
         nc.scalar.activation(out=std[:], in_=cols_early[:, : 2 * CT], func=ACT.Sqrt, bias=EPS)
 
-        half = NPOS // 2
-        quarter = NPOS // 4
-        interleave(nc.vector.tensor_copy, 0, 0, 3 * quarter)
-        interleave(nc.scalar.copy, 0, 3 * quarter, NPOS)
+        interleave(nc.vector.tensor_copy, 0, 0, 3 * QUARTER)
+        interleave(nc.scalar.copy, 0, 3 * QUARTER, NPOS)
         nc.vector.reciprocal(out=inv[:], in_=std[:])
         quantize(0, 0, 1)
-        interleave(nc.scalar.copy, 1, half, NPOS)
+        interleave(nc.scalar.copy, 1, HALF, NPOS)
         nc.vector.tensor_tensor(out=gain[:], in0=cols_early[:, 2 * CT : 4 * CT], in1=inv[:], op=ALU.mult)
-        interleave(nc.vector.tensor_copy, 1, 0, half)
+        interleave(nc.vector.tensor_copy, 1, 0, HALF)
         nc.vector.scalar_tensor_tensor(
             out=parts[:, :2, :].rearrange("p s i -> p (s i)"), in0=cols_early[:, 4 * CT : 6 * CT], scalar=-1.0,
             in1=gain[:], op0=ALU.mult, op1=ALU.mult,
@@ -205,7 +208,7 @@ def tile_bottleneck_transformer_pb_kernel(
         interleave(nc.vector.tensor_copy, 3, 0, NPOS)
 
         for n in range(EARLY_MAINS):
-            main_out(n, main_product(n, n % BANKS))
+            main_product(n, n % BANKS)
 
         bank = EARLY_MAINS % BANKS
         m = EARLY_MAINS
@@ -214,21 +217,21 @@ def tile_bottleneck_transformer_pb_kernel(
             bank = (bank + 1) % BANKS
             if n < PAIRED:
                 if n % 2 == 1:
-                    finish(n - 1, 2, "scalar" if n in (17, 21) else "gpsimd")
+                    finish(relu_gpsimd, n - 1, 2)
             elif n == TILES - 1:
-                finish(n, 1, "vector")
+                finish(relu_vector, n, 1)
             else:
-                finish(n, 1, "gpsimd" if n % 2 == 0 and n < TILES - 2 else "scalar")
-            if m < TILES and 3 * (m - EARLY_MAINS) // 2 == n:
-                main_out(m, main_product(m, bank))
+                finish(relu_scalar if n % 3 == 0 else relu_gpsimd, n, 1)
+            late = m - EARLY_MAINS
+            if m < TILES and n == 1 + 3 * late // 2:
+                main_product(m, bank)
                 bank = (bank + 1) % BANKS
-                piece = m - EARLY_MAINS
-                if piece < 4:
-                    interleave(nc.scalar.copy, 4, quarter * piece, quarter * (piece + 1))
                 m += 1
+                if late < 4:
+                    interleave(nc.scalar.copy, 4, QUARTER * late, QUARTER * (late + 1))
             if n == 0:
                 quantize(1, 0, 1)
-            elif n == 5:
+            elif n == COPY_AT:
                 interleave(nc.vector.tensor_copy, 5, 0, NPOS)
-            elif n == 9:
+            elif n == QUANTIZE_AT:
                 quantize(1, 1, 3)

from contextlib import ExitStack

import concourse.mybir as mybir
from concourse.masks import make_identity

B, CIN, CMID, COUT, NPOS = 2, 1024, 512, 2048, 512
EPS = 1e-5
FLOPS = 2 * B * COUT * NPOS * (CIN + CMID)

F32 = mybir.dt.float32
BF16 = mybir.dt.bfloat16
I32 = mybir.dt.int32
U32 = mybir.dt.uint32
U8 = mybir.dt.uint8
E5M2X4 = mybir.dt.float8_e5m2_x4
E2M1X4 = mybir.dt.float4_e2m1fn_x4
ALU = mybir.AluOpType
ACT = mybir.ActivationFunctionType

P = 128
PACK = 4
K_PASS = P * PACK
CT = COUT // P
TILES = B * CT
BANKS = 8
OPERANDS = 3
HALF = NPOS // 2
QUARTER = NPOS // 4
F32_MAX = 3.4028234663852886e38

HEAD_CT = 5
EARLY_MAINS = 12
PAIRED = 6
COPY_AT = 5
QUANTIZE_AT = 11


def tile_bottleneck_transformer_pb_kernel(
    tc, h_attn, x, conv3_w_words, conv3_w_scales, bn3_g, bn3_b, bn3_m, bn3_v,
    sc_w_words, sc_w_scales, sc_b, scbn_g, scbn_b, scbn_m, scbn_v, out,
):
    nc = tc.nc
    with ExitStack() as ctx:
        keep = ctx.enter_context(tc.tile_pool(name="keep", bufs=1))
        psum = ctx.enter_context(tc.psum_pool(name="psum", bufs=1))
        ctx.enter_context(tc.manual_schedule())

        raw = [keep.tile([P, PACK, NPOS], BF16, name="raw%d" % u, align_bytes=64) for u in range(OPERANDS * B)]
        grouped = [
            keep.tile([P, OPERANDS, NPOS, PACK], BF16, name="grouped%d" % b, align_bytes=64) for b in range(B)
        ]
        codes = [keep.tile([P, OPERANDS, NPOS], U32, name="codes%d" % b, align_bytes=64) for b in range(B)]
        scales = [keep.tile([P, OPERANDS, NPOS], U8, name="scales%d" % b, align_bytes=64) for b in range(B)]
        w_main = [keep.tile([P, COUT], U8, name="w_main%d" % h, align_bytes=64) for h in range(2)]
        w_short_head = keep.tile([P, 2, 2 * P * HEAD_CT], U8, align_bytes=64)
        w_short_rest = keep.tile([P, 2, 2 * P * (CT - HEAD_CT)], U8, align_bytes=64)
        plane_main = keep.tile([P, COUT], U8, align_bytes=64)
        plane_short_head = keep.tile([P, 2, P * HEAD_CT], U8, align_bytes=64)
        plane_short_rest = keep.tile([P, 2, P * (CT - HEAD_CT)], U8, align_bytes=64)
        rows = keep.tile([P, 2, P], BF16, align_bytes=64)
        ident = keep.tile([P, P], BF16, align_bytes=64)
        std = keep.tile([P, 2 * CT], F32)
        inv = keep.tile([P, 2 * CT], F32)
        gain = keep.tile([P, 2 * CT], F32)
        parts = keep.tile([P, 5, CT], F32)
        shift = keep.tile([P, CT], F32)
        res = keep.tile([P, TILES, NPOS], F32, align_bytes=64)

        def load_operand(u):
            b, s = divmod(u, OPERANDS)
            src = h_attn[b] if s == 0 else x[b, (s - 1) * K_PASS : s * K_PASS, :]
            nc.sync.dma_start(out=raw[u][:], in_=src.rearrange("(p t) n -> p t n", t=PACK))

        def load_vector(eng, group, place, vec):
            eng.dma_start(out=rows[CT * place : CT * (place + 1), group, :], in_=vec.rearrange("(i p) -> i p", p=P))

        def interleave(copy, u, n0, n1):
            copy(
                out=grouped[u // OPERANDS][:, u % OPERANDS, n0:n1, :].rearrange("p (c i) t -> p c t i", i=4),
                in_=raw[u][:, :, n0:n1].rearrange("p t (c i) -> p c t i", i=4),
            )

        def quantize(b, s0, s1):
            nc.vector.quantize_mx(
                out=codes[b][:, s0:s1, :].rearrange("p s n -> p (s n)").bitcast(E5M2X4),
                scales=scales[b][:, s0:s1, :].rearrange("p s n -> p (s n)"),
                in_=grouped[b][:, s0:s1, :, :].rearrange("p s n t -> p (s n t)"),
            )

        def main_product(n, bank):
            b, i = divmod(n, CT)
            h, j = divmod(i, CT // 2)
            acc = psum.tile([P, NPOS], F32, name="acc", tag="bank%d" % bank)
            nc.tensor.matmul_mx(
                out=acc[:],
                lhsT=w_main[h][:, 2 * P * j : 2 * P * (j + 1)].bitcast(E2M1X4),
                lhsT_scale=plane_main[:, P * i : P * (i + 1)],
                rhs=codes[b][:, 0, :].bitcast(E5M2X4),
                rhs_scale=scales[b][:, 0, :],
                start=True,
                stop=True,
            )
            nc.scalar.activation(
                out=res[:, n, :], in_=acc[:], func=ACT.Identity, scale=gain[:, i : i + 1], bias=shift[:, i : i + 1]
            )

        def short_product(n, bank):
            b, i = divmod(n, CT)
            acc = psum.tile([P, NPOS], F32, name="acc", tag="bank%d" % bank)
            if i < HEAD_CT:
                words, plane, j = w_short_head, plane_short_head, i
            else:
                words, plane, j = w_short_rest, plane_short_rest, i - HEAD_CT
            for g in range(2):
                nc.tensor.matmul_mx(
                    out=acc[:],
                    lhsT=words[:, g, 2 * P * j : 2 * P * (j + 1)].bitcast(E2M1X4),
                    lhsT_scale=plane[:, g, P * j : P * (j + 1)],
                    rhs=codes[b][:, 1 + g, :].bitcast(E5M2X4),
                    rhs_scale=scales[b][:, 1 + g, :],
                    start=(g == 0),
                    stop=(g == 1),
                )
            nc.vector.scalar_tensor_tensor(
                out=res[:, n, :], in0=acc[:], scalar=gain[:, CT + i : CT + i + 1], in1=res[:, n, :],
                op0=ALU.mult, op1=ALU.add,
            )

        def relu_scalar(vals):
            nc.scalar.activation(out=vals, in_=vals, func=ACT.Relu)

        def relu_vector(vals):
            nc.vector.tensor_scalar(out=vals, in0=vals, scalar1=0.0, scalar2=None, op0=ALU.max)

        def relu_gpsimd(vals):
            nc.gpsimd.tensor_scalar(out=vals, in0=vals, scalar1=F32_MAX, scalar2=0.0, op0=ALU.min, op1=ALU.max)

        def finish(relu, n, count):
            b, i = divmod(n, CT)
            relu(res[:, n : n + count, :].rearrange("p t n -> p (t n)"))
            nc.sync.dma_start(
                out=out[b, P * i : P * (i + count), :].rearrange("(t p) n -> p t n", p=P),
                in_=res[:, n : n + count, :],
            )

        nc.vector.memset(rows[96:, 0, :].bitcast(I32), 0)
        nc.vector.memset(rows[32:64, 1, :].bitcast(I32), 0)
        nc.vector.memset(rows[64:, 1, :].bitcast(I32), 0)
        nc.vector.memset(plane_main[:].bitcast(I32), 0)
        nc.vector.memset(plane_short_head[:].rearrange("p g n -> p (g n)").bitcast(I32), 0)
        nc.vector.memset(plane_short_rest[:].rearrange("p g n -> p (g n)").bitcast(I32), 0)
        make_identity(nc, ident[:])

        load_operand(0)
        for place, vec in enumerate((bn3_v, scbn_v, bn3_g, scbn_g, bn3_m, scbn_m)):
            load_vector(nc.sync, 0, place, vec)
        load_operand(1)
        load_vector(nc.gpsimd, 1, 1, scbn_b)
        load_vector(nc.gpsimd, 1, 2, sc_b)
        for r in range(4):
            nc.sync.dma_start(out=plane_main[r:P:32, :].bitcast(I32), in_=conv3_w_scales[0, r:16:4, :].bitcast(I32))
        load_vector(nc.sync, 1, 0, bn3_b)
        nc.sync.dma_start(out=w_main[0][:].bitcast(I32), in_=conv3_w_words[0, :, :COUT].bitcast(I32))
        load_operand(2)
        nc.sync.dma_start(out=w_main[1][:].bitcast(I32), in_=conv3_w_words[0, :, COUT:].bitcast(I32))
        load_operand(3)
        for words, plane, c0, c1 in (
            (w_short_head, plane_short_head, 0, P * HEAD_CT),
            (w_short_rest, plane_short_rest, P * HEAD_CT, COUT),
        ):
            nc.sync.dma_start(
                out=words[:].bitcast(I32),
                in_=sc_w_words[:, :, 2 * c0 : 2 * c1].rearrange("g p n -> p g n").bitcast(I32),
            )
            for r in range(4):
                nc.sync.dma_start(
                    out=plane[r:P:32, :, :].bitcast(I32),
                    in_=sc_w_scales[:, r:16:4, c0:c1].rearrange("g q n -> q g n").bitcast(I32),
                )
        load_operand(4)
        load_operand(5)

        cols_early = psum.tile([P, P], BF16, name="cols_early", tag="bank%d" % (BANKS - 2))
        cols_late = psum.tile([P, P], BF16, name="cols_late", tag="bank%d" % (BANKS - 1))
        nc.tensor.transpose(cols_early[:], rows[:, 0, :], ident[:])
        nc.tensor.transpose(cols_late[:], rows[:, 1, :], ident[:])
        nc.scalar.activation(out=std[:], in_=cols_early[:, : 2 * CT], func=ACT.Sqrt, bias=EPS)

        interleave(nc.vector.tensor_copy, 0, 0, 3 * QUARTER)
        interleave(nc.scalar.copy, 0, 3 * QUARTER, NPOS)
        nc.vector.reciprocal(out=inv[:], in_=std[:])
        quantize(0, 0, 1)
        interleave(nc.scalar.copy, 1, HALF, NPOS)
        nc.vector.tensor_tensor(out=gain[:], in0=cols_early[:, 2 * CT : 4 * CT], in1=inv[:], op=ALU.mult)
        interleave(nc.vector.tensor_copy, 1, 0, HALF)
        nc.vector.scalar_tensor_tensor(
            out=parts[:, :2, :].rearrange("p s i -> p (s i)"), in0=cols_early[:, 4 * CT : 6 * CT], scalar=-1.0,
            in1=gain[:], op0=ALU.mult, op1=ALU.mult,
        )
        nc.vector.tensor_tensor(out=parts[:, 2, :], in0=cols_late[:, 2 * CT : 3 * CT], in1=gain[:, CT:], op=ALU.mult)
        nc.vector.tensor_copy(out=parts[:, 3:, :].rearrange("p s i -> p (s i)"), in_=cols_late[:, : 2 * CT])
        nc.vector.tensor_reduce(
            out=shift[:], in_=parts[:].rearrange("p s i -> p i s"), axis=mybir.AxisListType.X, op=ALU.add
        )
        quantize(0, 1, 2)
        interleave(nc.vector.tensor_copy, 2, 0, NPOS)
        quantize(0, 2, 3)
        interleave(nc.vector.tensor_copy, 3, 0, NPOS)

        for n in range(EARLY_MAINS):
            main_product(n, n % BANKS)

        bank = EARLY_MAINS % BANKS
        m = EARLY_MAINS
        for n in range(TILES):
            short_product(n, bank)
            bank = (bank + 1) % BANKS
            if n < PAIRED:
                if n % 2 == 1:
                    finish(relu_gpsimd, n - 1, 2)
            elif n == TILES - 1:
                finish(relu_vector, n, 1)
            else:
                finish(relu_scalar if n % 3 == 0 else relu_gpsimd, n, 1)
            late = m - EARLY_MAINS
            if m < TILES and n == 1 + 3 * late // 2:
                main_product(m, bank)
                bank = (bank + 1) % BANKS
                m += 1
                if late < 4:
                    interleave(nc.scalar.copy, 4, QUARTER * late, QUARTER * (late + 1))
            if n == 0:
                quantize(1, 0, 1)
            elif n == COPY_AT:
                interleave(nc.vector.tensor_copy, 5, 0, NPOS)
            elif n == QUANTIZE_AT:
                quantize(1, 1, 3)
